import numpy as np
import ml_dtypes


def mxq(x, axis, fmt="e4m3"):
    dtype, down = {"e4m3": (ml_dtypes.float8_e4m3fn, 7), "e5m2": (ml_dtypes.float8_e5m2, 14)}[fmt]
    v = np.moveaxis(np.asarray(x, np.float32).astype(ml_dtypes.bfloat16).astype(np.float64), axis, -1)
    blocks = v.reshape(v.shape[:-1] + (-1, 32))
    amax = np.abs(blocks).max(-1, keepdims=True)
    byte = np.maximum(np.where(amax > 0, np.frexp(amax)[1] - 1 + 127, 0) - down, 1)
    scale = np.exp2(byte - 127.0)
    codes = (blocks / scale).astype(np.float32).astype(dtype).astype(np.float64)
    return np.moveaxis((codes * scale).reshape(v.shape), -1, axis)


WIDE = False


def mx_kscale(k):
    if not WIDE:
        return np.ones(k)
    levels = np.array([10, -10, 5, -5, 0])
    a = np.random.permutation(np.resize(levels, k // 512 * 4)).reshape(k // 512, 4)
    idx = np.arange(k)
    return np.exp2(a[idx // 512, idx % 128 // 32])


BF16 = ml_dtypes.bfloat16


def bf(x):
    return np.asarray(x, np.float32).astype(BF16)


def f64(x):
    return np.asarray(x).astype(np.float64)


E2M1 = np.array([0.0, 0.5, 1.0, 1.5, 2.0, 3.0, 4.0, 6.0, -0.0, -0.5, -1.0, -1.5, -2.0, -3.0, -4.0, -6.0])


def pack_weight(w, fmt):
    k, n = w.shape
    w = f64(bf(w)).reshape(k // 32, 32, n)
    amax = np.abs(w).max(1)
    if fmt == "e4m3":
        byte = np.frexp(amax)[1] - 1 + 127 - 7
    else:
        mant, ex = np.frexp(amax / 6.0)
        byte = np.where(mant > 0.5, ex, ex - 1) + 127
    byte = np.clip(np.where(amax > 0, byte, 1), 1, 254)
    scaled = (w * np.exp2(127.0 - byte)[:, None, :]).reshape(k, n).astype(np.float32)
    by_word = np.ascontiguousarray(scaled.reshape(k // 512, 128, 4, n).transpose(0, 1, 3, 2))
    if fmt == "e4m3":
        words = by_word.astype(ml_dtypes.float8_e4m3fn).view(np.uint8)
    else:
        c = by_word.astype(ml_dtypes.float4_e2m1fn).view(np.uint8) & 0xF
        words = c[..., 0::2] | (c[..., 1::2] << 4)
    return np.ascontiguousarray(words), np.ascontiguousarray(byte.astype(np.uint8).reshape(k // 512, 16, n))


def unpack_weight(words, scales, fmt):
    g, p, n, _ = words.shape
    if fmt == "e4m3":
        vals = np.ascontiguousarray(words).view(ml_dtypes.float8_e4m3fn).astype(np.float64)
    else:
        nib = np.empty((g, p, n, 4), np.uint8)
        nib[..., 0::2] = words & 0xF
        nib[..., 1::2] = words >> 4
        vals = E2M1[nib]
    vals = vals * np.repeat(np.exp2(scales.astype(np.float64) - 127.0), 8, axis=1)[..., None]
    return vals.transpose(0, 1, 3, 2).reshape(g * 512, n)


S, B, H, NC, DC = 512, 16, 512, 8, 64
ROUTINGS = 4
E = 1


def squash(x, axis=-1):
    s = np.sum(x * x, axis=axis, keepdims=True)
    return x / np.sqrt(s + 1e-7)


def softmax(v, axis):
    e = np.exp(v - v.max(axis=axis, keepdims=True))
    return e / e.sum(axis=axis, keepdims=True)


def setup_inputs():
    s = mx_kscale(H)
    std = np.sqrt(2.0 / (H + NC * DC))
    inputs = bf(np.random.standard_normal((S, B, H)) * s)
    stack = np.random.standard_normal((E, H, NC * DC)) * std / s[None, :, None]
    words, scales = pack_weight(stack.reshape(-1, NC * DC), "e4m3")
    return {"inputs": inputs, "W_words": words, "W_scales": scales}


def reference(inputs, W_words, W_scales):
    x = np.transpose(f64(inputs), (1, 0, 2))
    w = unpack_weight(W_words, W_scales, "e4m3").reshape(E, H, NC * DC)
    u = mxq(x, 2, "e4m3") @ w[0]
    u = u.reshape(B, S, NC, DC)
    u = np.transpose(u, (0, 2, 1, 3))
    b = np.zeros((B, NC, S, 1))
    outputs = None
    for i in range(ROUTINGS):
        c = softmax(b, 1)
        outputs = squash(np.sum(c * u, axis=2))
        if i < ROUTINGS - 1:
            update = np.sum(outputs[:, :, None, :] * u, axis=-1, keepdims=True)
            b = b + update
    return outputs

@@ -1,0 +1,314 @@
+from contextlib import ExitStack
+
+import concourse.mybir as mybir
+from concourse.masks import make_identity
+
+F32 = mybir.dt.float32
+BF16 = mybir.dt.bfloat16
+I32 = mybir.dt.int32
+U32 = mybir.dt.uint32
+U8 = mybir.dt.uint8
+FP8X4 = mybir.dt.float8_e4m3fn_x4
+ALU = mybir.AluOpType
+ACT = mybir.ActivationFunctionType
+AX = mybir.AxisListType
+
+S, B, H, NC, DC = 512, 16, 512, 8, 64
+ROUTINGS = 4
+P = 128
+SC = S // P
+NJ = NC * DC // P
+Q = P // NC
+R = 4
+M = P // R
+GB = 4
+NG = B // GB
+PHASES = 2 * ROUTINGS - 1
+
+FLOPS = 2 * S * B * H * NC * DC + (2 * ROUTINGS - 1) * 2 * S * B * NC * DC
+
+
+def tile_capsule_t_e_kernel(tc, inputs, W_words, W_scales, out):
+    nc = tc.nc
+    with ExitStack() as ctx:
+        const = ctx.enter_context(tc.tile_pool(name="const", bufs=1))
+        upool = ctx.enter_context(tc.tile_pool(name="upool", bufs=1))
+        xpool = ctx.enter_context(tc.tile_pool(name="xpool", bufs=2))
+        qpool = ctx.enter_context(tc.tile_pool(name="qpool", bufs=2))
+        prodpool = ctx.enter_context(tc.tile_pool(name="prodpool", bufs=2 * NJ))
+        reppool = ctx.enter_context(tc.tile_pool(name="reppool", bufs=2))
+        junkpool = ctx.enter_context(tc.tile_pool(name="junkpool", bufs=4))
+        small = ctx.enter_context(tc.tile_pool(name="small", bufs=3))
+        psum_a = ctx.enter_context(tc.psum_pool(name="psum_a", bufs=4))
+        psum_b = ctx.enter_context(tc.psum_pool(name="psum_b", bufs=3))
+        psum_s = ctx.enter_context(tc.psum_pool(name="psum_s", bufs=1))
+
+        ident = const.tile([P, P], F32)
+        make_identity(nc, ident[:])
+        capsule_of = const.tile([P, NC], F32)
+        nc.vector.tensor_reduce(
+            out=capsule_of[:], in_=ident[:].rearrange("p (n q) -> p n q", q=Q), axis=AX.X, op=ALU.add
+        )
+        same_capsule = const.tile([P, NC, Q], F32)
+        nc.vector.tensor_copy(out=same_capsule[:], in_=capsule_of[:].unsqueeze(2).to_broadcast([P, NC, Q]))
+        neg_half = const.tile([P, GB], F32)
+        nc.vector.memset(neg_half[:], -0.5)
+        o_all = const.tile([P, (NJ - 1) * B + P], F32)
+        nc.vector.memset(o_all[:], 0.0)
+        usum = const.tile([P, NJ, B], F32)
+
+        w_raw = const.tile([P, NC * DC], U32)
+        nc.sync.dma_start(out=w_raw[:].bitcast(I32), in_=W_words[0].rearrange("p n t -> p (n t)").bitcast(I32))
+        plane_raw = const.tile([P, NC * DC], U8)
+        nc.vector.memset(plane_raw[:].bitcast(I32), 0)
+        for quad in range(4):
+            nc.sync.dma_start(
+                out=plane_raw[32 * quad : 32 * quad + 4, :].bitcast(I32),
+                in_=W_scales[0, 4 * quad : 4 * quad + 4, :].bitcast(I32),
+            )
+        w_words = const.tile([P, NC * DC], U32, align_bytes=64)
+        nc.vector.tensor_copy(
+            out=w_words[:].bitcast(I32).rearrange("p (j m r) -> p j m r", j=NJ, r=R),
+            in_=w_raw[:].bitcast(I32).rearrange("p (m j r) -> p j m r", j=NJ, r=R),
+        )
+        w_plane = const.tile([P, NC * DC], U8, align_bytes=64)
+        nc.vector.tensor_copy(
+            out=w_plane[:].bitcast(I32).rearrange("p (j m) -> p j m", j=NJ),
+            in_=plane_raw[:].bitcast(I32).rearrange("p (m j) -> p j m", j=NJ),
+        )
+
+        u = []
+        for b in range(B):
+            u_b = upool.tile([P, NJ, S], F32, name="u%d" % b)
+            u.append(u_b)
+        osum = []
+        for g in range(NG):
+            osum_g = const.tile([P, NJ, GB], F32, name="osum%d" % g)
+            osum.append(osum_g)
+        live = {}
+
+        def project(g):
+            x_g = xpool.tile([P, SC, GB, H], BF16)
+            nc.sync.dma_start(
+                out=x_g[:], in_=inputs[:, g * GB : (g + 1) * GB, :].rearrange("(c p) b h -> p c b h", p=P)
+            )
+            for bi in range(GB):
+                b = g * GB + bi
+                grouped = qpool.tile([P, S, 4], BF16, align_bytes=64)
+                for half in range(SC // 2):
+                    xt = psum_b.tile([P, 2, 2, P], F32, tag="b")
+                    for c in range(2):
+                        words = x_g[:, 2 * half + c, bi, :].bitcast(F32)
+                        for w in range(2):
+                            nc.tensor.transpose(xt[:, c, w, :], words[:, w : H // 2 : 2], ident[:])
+                    nc.scalar.copy(
+                        out=grouped[:]
+                        .bitcast(F32)[:, 2 * half * P : 2 * (half + 1) * P, :]
+                        .rearrange("p (c s) w -> p c s w", c=2),
+                        in_=xt[:].rearrange("p c w s -> p c s w"),
+                    )
+                codes = qpool.tile([P, S], U32, align_bytes=64)
+                plane = qpool.tile([P, S], U8, align_bytes=64)
+                nc.vector.quantize_mx(
+                    out=codes[:].bitcast(FP8X4), scales=plane[:], in_=grouped[:].rearrange("p s t -> p (s t)")
+                )
+                for j in range(NJ):
+                    acc = psum_a.tile([P, S], F32, tag="a")
+                    nc.tensor.matmul_mx(
+                        out=acc[:],
+                        lhsT=w_words[:, j * P : (j + 1) * P].bitcast(FP8X4),
+                        lhsT_scale=w_plane[:, j * P : (j + 1) * P],
+                        rhs=codes[:].bitcast(FP8X4),
+                        rhs_scale=plane[:],
+                        start=True,
+                        stop=True,
+                    )
+                    if j % 2 == 0:
+                        nc.scalar.activation(
+                            out=u[b][:, j, :], in_=acc[:], func=ACT.Copy, accum_out=usum[:, j, b : b + 1]
+                        )
+                    else:
+                        nc.vector.tensor_scalar(
+                            out=u[b][:, j, :],
+                            in0=acc[:],
+                            scalar1=1.0,
+                            scalar2=None,
+                            op0=ALU.mult,
+                            op1=ALU.add,
+                            accum_out=usum[:, j, b : b + 1],
+                        )
+            v = small.tile([P, NJ, GB], F32)
+            nc.vector.tensor_scalar(
+                out=v[:], in0=usum[:, :, g * GB : (g + 1) * GB], scalar1=1.0 / NC, scalar2=None, op0=ALU.mult
+            )
+            live[("v", g)] = v
+
+        def norm(g):
+            v = live[("v", g)]
+            sq = small.tile([P, NJ, GB], F32)
+            nc.vector.tensor_tensor(out=sq[:], in0=v[:], in1=v[:], op=ALU.mult)
+            ss = psum_s.tile([P, GB], F32, tag="s")
+            for j in range(NJ):
+                nc.tensor.matmul(
+                    out=ss[:],
+                    lhsT=same_capsule[:].rearrange("p n q -> p (n q)"),
+                    rhs=sq[:, j, :],
+                    start=(j == 0),
+                    stop=(j == NJ - 1),
+                )
+            sse = small.tile([P, GB], F32)
+            nc.scalar.activation(out=sse[:], in_=ss[:], func=ACT.Copy, bias=1e-7)
+            rs = small.tile([P, GB], F32)
+            nc.gpsimd.tensor_tensor(out=rs[:], in0=sse[:], in1=neg_half[:], op=ALU.pow)
+            live[("rs", g)] = rs
+
+        def squash(g, rnd):
+            v = live[("v", g)]
+            rs_b = live[("rs", g)][:].unsqueeze(1).to_broadcast([P, NJ, GB])
+            if rnd == 0:
+                nc.vector.tensor_tensor(out=osum[g][:], in0=v[:], in1=rs_b, op=ALU.mult)
+            elif rnd < ROUTINGS - 1:
+                o = small.tile([P, NJ, GB], F32)
+                nc.vector.tensor_tensor(out=o[:], in0=v[:], in1=rs_b, op=ALU.mult)
+                nc.vector.tensor_tensor(out=osum[g][:], in0=osum[g][:], in1=o[:], op=ALU.add)
+            else:
+                nc.vector.tensor_tensor(
+                    out=o_all[:, 0 : NJ * B].rearrange("p (j b) -> p j b", j=NJ)[:, :, g * GB : (g + 1) * GB],
+                    in0=v[:],
+                    in1=rs_b,
+                    op=ALU.mult,
+                )
+
+        def logit_products(g):
+            for bi in range(GB):
+                b = g * GB + bi
+                prods = []
+                for j in range(NJ):
+                    prod = prodpool.tile([P, S], F32)
+                    if j % 2 == 0:
+                        nc.scalar.activation(
+                            out=prod[:], in_=u[b][:, j, :], func=ACT.Copy, scale=osum[g][:, j, bi : bi + 1]
+                        )
+                    else:
+                        nc.gpsimd.tensor_scalar(
+                            out=prod[:],
+                            in0=u[b][:, j, :],
+                            scalar1=osum[g][:, j, bi : bi + 1],
+                            scalar2=0.0,
+                            op0=ALU.mult,
+                            op1=ALU.add,
+                        )
+                    prods.append(prod)
+                part = psum_a.tile([P, SC, P], F32, tag="a")
+                for c in range(SC):
+                    for j in range(NJ):
+                        nc.tensor.matmul(
+                            out=part[:, c, :],
+                            lhsT=prods[j][:, c * P : (c + 1) * P],
+                            rhs=ident[:],
+                            start=(j == 0),
+                            stop=(j == NJ - 1),
+                            is_transpose=True,
+                        )
+                live[("part", b)] = part
+
+        def softmax_exp(g):
+            t = small.tile([P, GB * SC, NC], F32)
+            for bi in range(GB):
+                nc.vector.tensor_reduce(
+                    out=t[:, bi * SC : (bi + 1) * SC, :],
+                    in_=live[("part", g * GB + bi)][:].rearrange("p c (n q) -> p c n q", q=Q),
+                    axis=AX.X,
+                    op=ALU.add,
+                )
+            tmax = small.tile([P, GB * SC], F32)
+            nc.vector.tensor_reduce(out=tmax[:], in_=t[:], axis=AX.X, op=ALU.max)
+            shifted = small.tile([P, GB * SC, NC], F32)
+            nc.vector.tensor_tensor(
+                out=shifted[:], in0=t[:], in1=tmax[:].unsqueeze(2).to_broadcast([P, GB * SC, NC]), op=ALU.subtract
+            )
+            e = small.tile([P, GB * SC, NC], F32)
+            nc.scalar.activation(out=e[:], in_=shifted[:], func=ACT.Exp)
+            live[("e", g)] = e
+
+        def spread(g, bi):
+            c_n = live[("c", g)]
+            rep = reppool.tile([P, SC, NC, Q], F32)
+            nc.scalar.activation(
+                out=rep[:],
+                in_=c_n[:, bi * SC : (bi + 1) * SC, :].unsqueeze(3).to_broadcast([P, SC, NC, Q]),
+                func=ACT.Copy,
+            )
+            c_t = psum_b.tile([P, SC, P], F32, tag="b")
+            for c in range(SC):
+                nc.tensor.transpose(c_t[:, c, :], rep[:, c, :, :].rearrange("p n q -> p (n q)"), ident[:])
+            live[("c_t", g * GB + bi)] = c_t
+
+        def softmax_norm(g):
+            e = live[("e", g)]
+            z = small.tile([P, GB * SC], F32)
+            nc.vector.tensor_reduce(out=z[:], in_=e[:], axis=AX.X, op=ALU.add)
+            rz = small.tile([P, GB * SC], F32)
+            nc.vector.reciprocal(out=rz[:], in_=z[:])
+            c_n = small.tile([P, GB * SC, NC], F32)
+            nc.vector.tensor_tensor(
+                out=c_n[:], in0=e[:], in1=rz[:].unsqueeze(2).to_broadcast([P, GB * SC, NC]), op=ALU.mult
+            )
+            live[("c", g)] = c_n
+            spread(g, 0)
+
+        def weighted_sums(g):
+            v = small.tile([P, NJ, GB], F32)
+            for bi in range(GB):
+                b = g * GB + bi
+                if bi + 1 < GB:
+                    spread(g, bi + 1)
+                for j in range(NJ):
+                    junk = junkpool.tile([P, S], F32)
+                    nc.vector.scalar_tensor_tensor(
+                        out=junk[:],
+                        in0=u[b][:, j, :],
+                        scalar=1.0,
+                        in1=live[("c_t", b)][:].rearrange("p c s -> p (c s)"),
+                        op0=ALU.mult,
+                        op1=ALU.mult,
+                        accum_out=v[:, j, bi : bi + 1],
+                    )
+            live[("v", g)] = v
+
+        steps = [(t - g, g) for t in range(PHASES + NG - 1) for g in range(NG)]
+
+        def valid(pos):
+            return 0 <= pos < len(steps) and 0 <= steps[pos][0] < PHASES
+
+        for pos in range(len(steps) + 2):
+            if valid(pos - 2):
+                phase, g = steps[pos - 2]
+                if phase % 2 == 1:
+                    softmax_norm(g)
+                else:
+                    squash(g, phase // 2)
+            if valid(pos - 1):
+                phase, g = steps[pos - 1]
+                if phase % 2 == 1:
+                    softmax_exp(g)
+                else:
+                    norm(g)
+            if valid(pos):
+                phase, g = steps[pos]
+                if phase == 0:
+                    project(g)
+                elif phase % 2 == 1:
+                    logit_products(g)
+                else:
+                    weighted_sums(g)
+
+        o_t = psum_s.tile([P, NJ, P], F32, tag="s")
+        for j in range(NJ):
+            nc.tensor.transpose(o_t[:, j, :], o_all[:, j * B : j * B + P], ident[:])
+        res = small.tile([B, NC * DC], F32)
+        nc.scalar.copy(
+            out=res[:].rearrange("b (m j r) -> b m j r", j=NJ, r=R),
+            in_=o_t[0:B].rearrange("b j (m r) -> b m j r", r=R),
+        )
+        nc.sync.dma_start(out=out.rearrange("b n d -> b (n d)"), in_=res[:])

@@ -23,7 +23,7 @@ R = 4
 M = P // R
 GB = 4
 NG = B // GB
-PHASES = 2 * ROUTINGS - 1
+STEPS = ROUTINGS * B
 
 FLOPS = 2 * S * B * H * NC * DC + (2 * ROUTINGS - 1) * 2 * S * B * NC * DC
 
@@ -33,7 +33,7 @@ def tile_capsule_t_e_kernel(tc, inputs, W_words, W_scales, out):
     with ExitStack() as ctx:
         const = ctx.enter_context(tc.tile_pool(name="const", bufs=1))
         upool = ctx.enter_context(tc.tile_pool(name="upool", bufs=1))
-        xpool = ctx.enter_context(tc.tile_pool(name="xpool", bufs=2))
+        xpool = ctx.enter_context(tc.tile_pool(name="xpool", bufs=4))
         qpool = ctx.enter_context(tc.tile_pool(name="qpool", bufs=2))
         prodpool = ctx.enter_context(tc.tile_pool(name="prodpool", bufs=2 * NJ))
         reppool = ctx.enter_context(tc.tile_pool(name="reppool", bufs=2))
@@ -42,6 +42,7 @@ def tile_capsule_t_e_kernel(tc, inputs, W_words, W_scales, out):
         psum_a = ctx.enter_context(tc.psum_pool(name="psum_a", bufs=4))
         psum_b = ctx.enter_context(tc.psum_pool(name="psum_b", bufs=3))
         psum_s = ctx.enter_context(tc.psum_pool(name="psum_s", bufs=1))
+        ctx.enter_context(tc.manual_schedule())
 
         ident = const.tile([P, P], F32)
         make_identity(nc, ident[:])
@@ -87,82 +88,154 @@ def tile_capsule_t_e_kernel(tc, inputs, W_words, W_scales, out):
             osum.append(osum_g)
         live = {}
 
-        def project(g):
-            x_g = xpool.tile([P, SC, GB, H], BF16)
-            nc.sync.dma_start(
-                out=x_g[:], in_=inputs[:, g * GB : (g + 1) * GB, :].rearrange("(c p) b h -> p c b h", p=P)
-            )
-            for bi in range(GB):
-                b = g * GB + bi
-                grouped = qpool.tile([P, S, 4], BF16, align_bytes=64)
-                for half in range(SC // 2):
-                    xt = psum_b.tile([P, 2, 2, P], F32, tag="b")
-                    for c in range(2):
-                        words = x_g[:, 2 * half + c, bi, :].bitcast(F32)
-                        for w in range(2):
-                            nc.tensor.transpose(xt[:, c, w, :], words[:, w : H // 2 : 2], ident[:])
-                    nc.scalar.copy(
-                        out=grouped[:]
-                        .bitcast(F32)[:, 2 * half * P : 2 * (half + 1) * P, :]
-                        .rearrange("p (c s) w -> p c s w", c=2),
-                        in_=xt[:].rearrange("p c w s -> p c s w"),
-                    )
-                codes = qpool.tile([P, S], U32, align_bytes=64)
-                plane = qpool.tile([P, S], U8, align_bytes=64)
-                nc.vector.quantize_mx(
-                    out=codes[:].bitcast(FP8X4), scales=plane[:], in_=grouped[:].rearrange("p s t -> p (s t)")
-                )
-                for j in range(NJ):
-                    acc = psum_a.tile([P, S], F32, tag="a")
-                    nc.tensor.matmul_mx(
-                        out=acc[:],
-                        lhsT=w_words[:, j * P : (j + 1) * P].bitcast(FP8X4),
-                        lhsT_scale=w_plane[:, j * P : (j + 1) * P],
-                        rhs=codes[:].bitcast(FP8X4),
-                        rhs_scale=plane[:],
-                        start=True,
-                        stop=True,
-                    )
-                    if j % 2 == 0:
-                        nc.scalar.activation(
-                            out=u[b][:, j, :], in_=acc[:], func=ACT.Copy, accum_out=usum[:, j, b : b + 1]
-                        )
-                    else:
-                        nc.vector.tensor_scalar(
-                            out=u[b][:, j, :],
-                            in0=acc[:],
-                            scalar1=1.0,
-                            scalar2=None,
-                            op0=ALU.mult,
-                            op1=ALU.add,
-                            accum_out=usum[:, j, b : b + 1],
-                        )
-            v = small.tile([P, NJ, GB], F32)
-            nc.vector.tensor_scalar(
-                out=v[:], in0=usum[:, :, g * GB : (g + 1) * GB], scalar1=1.0 / NC, scalar2=None, op0=ALU.mult
-            )
-            live[("v", g)] = v
+        def in_round_0(m):
+            return 0 <= m < B
 
-        def norm(g):
+        def in_later_round(m):
+            return B <= m < STEPS
+
+        def ends_group(m):
+            return 0 <= m < STEPS and m % GB == GB - 1
+
+        def feeds_a_round(m):
+            return 0 <= m < STEPS - B
+
+        def load(m):
+            x_b = xpool.tile([P, SC, H], BF16)
+            nc.sync.dma_start(out=x_b[:], in_=inputs[:, m, :].rearrange("(c p) h -> p c h", p=P))
+            live[("x", m)] = x_b
+
+        def transpose_x(m):
+            x_b = live[("x", m)]
+            grouped = qpool.tile([P, S, 4], BF16, align_bytes=64)
+            for half in range(SC // 2):
+                xt = psum_b.tile([P, 2, 2, P], F32, tag="b")
+                for c in range(2):
+                    words = x_b[:, 2 * half + c, :].bitcast(F32)
+                    for w in range(2):
+                        nc.tensor.transpose(xt[:, c, w, :], words[:, w : H // 2 : 2], ident[:])
+                dst = grouped[:].bitcast(F32)[:, 2 * half * P : 2 * (half + 1) * P, :]
+                if half == 0:
+                    nc.scalar.copy(
+                        out=dst.rearrange("p (c s) w -> p c s w", c=2), in_=xt[:].rearrange("p c w s -> p c s w")
+                    )
+                else:
+                    nc.vector.tensor_copy(
+                        out=dst.rearrange("p (c s) w -> p c s w", c=2), in_=xt[:].rearrange("p c w s -> p c s w")
+                    )
+            live[("grouped", m)] = grouped
+
+        def quantise(m):
+            codes = qpool.tile([P, S], U32, align_bytes=64)
+            plane = qpool.tile([P, S], U8, align_bytes=64)
+            nc.vector.quantize_mx(
+                out=codes[:].bitcast(FP8X4),
+                scales=plane[:],
+                in_=live[("grouped", m)][:].rearrange("p s t -> p (s t)"),
+            )
+            live[("codes", m)] = (codes, plane)
+
+        def project(m):
+            codes, plane = live[("codes", m)]
+            for j in range(NJ):
+                acc = psum_a.tile([P, S], F32, tag="a")
+                nc.tensor.matmul_mx(
+                    out=acc[:],
+                    lhsT=w_words[:, j * P : (j + 1) * P].bitcast(FP8X4),
+                    lhsT_scale=w_plane[:, j * P : (j + 1) * P],
+                    rhs=codes[:].bitcast(FP8X4),
+                    rhs_scale=plane[:],
+                    start=True,
+                    stop=True,
+                )
+                if j % 2 == 0:
+                    nc.scalar.activation(
+                        out=u[m][:, j, :], in_=acc[:], func=ACT.Copy, accum_out=usum[:, j, m : m + 1]
+                    )
+                else:
+                    nc.vector.tensor_scalar(
+                        out=u[m][:, j, :],
+                        in0=acc[:],
+                        scalar1=1.0,
+                        scalar2=None,
+                        op0=ALU.mult,
+                        op1=ALU.add,
+                        accum_out=usum[:, j, m : m + 1],
+                    )
+
+        def replicate(m):
+            bi = m % GB
+            c_n = live[("c", m % B // GB)]
+            rep = reppool.tile([P, SC, NC, Q], F32)
+            nc.scalar.activation(
+                out=rep[:],
+                in_=c_n[:, bi * SC : (bi + 1) * SC, :].unsqueeze(3).to_broadcast([P, SC, NC, Q]),
+                func=ACT.Copy,
+            )
+            live[("rep", m)] = rep
+
+        def transpose_c(m):
+            rep = live[("rep", m)]
+            c_t = psum_b.tile([P, SC, P], F32, tag="b")
+            for c in range(SC):
+                nc.tensor.transpose(c_t[:, c, :], rep[:, c, :, :].rearrange("p n q -> p (n q)"), ident[:])
+            live[("c_t", m)] = c_t
+
+        def sums(m):
+            b = m % B
+            if b % GB == 0:
+                v_new = small.tile([P, NJ, GB], F32, tag="v")
+                live[("v", b // GB)] = v_new
+            v = live[("v", b // GB)]
+            for j in range(NJ):
+                junk = junkpool.tile([P, S], F32)
+                nc.vector.scalar_tensor_tensor(
+                    out=junk[:],
+                    in0=u[b][:, j, :],
+                    scalar=1.0,
+                    in1=live[("c_t", m)][:].rearrange("p c s -> p (c s)"),
+                    op0=ALU.mult,
+                    op1=ALU.mult,
+                    accum_out=v[:, j, b % GB : b % GB + 1],
+                )
+
+        def square(m):
+            g = m % B // GB
+            if m < B:
+                v_first = small.tile([P, NJ, GB], F32, tag="v")
+                nc.vector.tensor_scalar(
+                    out=v_first[:], in0=usum[:, :, g * GB : (g + 1) * GB], scalar1=1.0 / NC, scalar2=None, op0=ALU.mult
+                )
+                live[("v", g)] = v_first
             v = live[("v", g)]
             sq = small.tile([P, NJ, GB], F32)
             nc.vector.tensor_tensor(out=sq[:], in0=v[:], in1=v[:], op=ALU.mult)
+            live[("sq", g)] = sq
+
+        def capsule_sums(m):
+            g = m % B // GB
             ss = psum_s.tile([P, GB], F32, tag="s")
             for j in range(NJ):
                 nc.tensor.matmul(
                     out=ss[:],
                     lhsT=same_capsule[:].rearrange("p n q -> p (n q)"),
-                    rhs=sq[:, j, :],
+                    rhs=live[("sq", g)][:, j, :],
                     start=(j == 0),
                     stop=(j == NJ - 1),
                 )
+            live[("ss", g)] = ss
+
+        def inverse_root(m):
+            g = m % B // GB
             sse = small.tile([P, GB], F32)
-            nc.scalar.activation(out=sse[:], in_=ss[:], func=ACT.Copy, bias=1e-7)
+            nc.scalar.activation(out=sse[:], in_=live[("ss", g)][:], func=ACT.Copy, bias=1e-7)
             rs = small.tile([P, GB], F32)
             nc.gpsimd.tensor_tensor(out=rs[:], in0=sse[:], in1=neg_half[:], op=ALU.pow)
             live[("rs", g)] = rs
 
-        def squash(g, rnd):
+        def squash(m):
+            g = m % B // GB
+            rnd = m // B
             v = live[("v", g)]
             rs_b = live[("rs", g)][:].unsqueeze(1).to_broadcast([P, NJ, GB])
             if rnd == 0:
@@ -179,72 +252,73 @@ def tile_capsule_t_e_kernel(tc, inputs, W_words, W_scales, out):
                     op=ALU.mult,
                 )
 
-        def logit_products(g):
-            for bi in range(GB):
-                b = g * GB + bi
-                prods = []
-                for j in range(NJ):
-                    prod = prodpool.tile([P, S], F32)
-                    if j % 2 == 0:
-                        nc.scalar.activation(
-                            out=prod[:], in_=u[b][:, j, :], func=ACT.Copy, scale=osum[g][:, j, bi : bi + 1]
-                        )
-                    else:
-                        nc.gpsimd.tensor_scalar(
-                            out=prod[:],
-                            in0=u[b][:, j, :],
-                            scalar1=osum[g][:, j, bi : bi + 1],
-                            scalar2=0.0,
-                            op0=ALU.mult,
-                            op1=ALU.add,
-                        )
-                    prods.append(prod)
-                part = psum_a.tile([P, SC, P], F32, tag="a")
-                for c in range(SC):
-                    for j in range(NJ):
-                        nc.tensor.matmul(
-                            out=part[:, c, :],
-                            lhsT=prods[j][:, c * P : (c + 1) * P],
-                            rhs=ident[:],
-                            start=(j == 0),
-                            stop=(j == NJ - 1),
-                            is_transpose=True,
-                        )
-                live[("part", b)] = part
+        def products(m):
+            b = m % B
+            prods = []
+            for j in range(NJ):
+                prod = prodpool.tile([P, S], F32)
+                if j % 2 == 0:
+                    nc.scalar.activation(
+                        out=prod[:], in_=u[b][:, j, :], func=ACT.Copy, scale=osum[b // GB][:, j, b % GB : b % GB + 1]
+                    )
+                else:
+                    nc.gpsimd.tensor_scalar(
+                        out=prod[:],
+                        in0=u[b][:, j, :],
+                        scalar1=osum[b // GB][:, j, b % GB : b % GB + 1],
+                        scalar2=0.0,
+                        op0=ALU.mult,
+                        op1=ALU.add,
+                    )
+                prods.append(prod)
+            live[("prods", m)] = prods
 
-        def softmax_exp(g):
-            t = small.tile([P, GB * SC, NC], F32)
-            for bi in range(GB):
-                nc.vector.tensor_reduce(
-                    out=t[:, bi * SC : (bi + 1) * SC, :],
-                    in_=live[("part", g * GB + bi)][:].rearrange("p c (n q) -> p c n q", q=Q),
-                    axis=AX.X,
-                    op=ALU.add,
-                )
+        def transpose_products(m):
+            prods = live[("prods", m)]
+            part = psum_a.tile([P, SC, P], F32, tag="a")
+            for c in range(SC):
+                for j in range(NJ):
+                    nc.tensor.matmul(
+                        out=part[:, c, :],
+                        lhsT=prods[j][:, c * P : (c + 1) * P],
+                        rhs=ident[:],
+                        start=(j == 0),
+                        stop=(j == NJ - 1),
+                        is_transpose=True,
+                    )
+            live[("part", m)] = part
+
+        def logits(m):
+            b = m % B
+            if b % GB == 0:
+                t_new = small.tile([P, GB * SC, NC], F32, tag="t")
+                live[("t", b // GB)] = t_new
+            nc.vector.tensor_reduce(
+                out=live[("t", b // GB)][:, b % GB * SC : (b % GB + 1) * SC, :],
+                in_=live[("part", m)][:].rearrange("p c (n q) -> p c n q", q=Q),
+                axis=AX.X,
+                op=ALU.add,
+            )
+
+        def shift(m):
+            g = m % B // GB
+            t = live[("t", g)]
             tmax = small.tile([P, GB * SC], F32)
             nc.vector.tensor_reduce(out=tmax[:], in_=t[:], axis=AX.X, op=ALU.max)
             shifted = small.tile([P, GB * SC, NC], F32)
             nc.vector.tensor_tensor(
                 out=shifted[:], in0=t[:], in1=tmax[:].unsqueeze(2).to_broadcast([P, GB * SC, NC]), op=ALU.subtract
             )
+            live[("shifted", g)] = shifted
+
+        def exponent(m):
+            g = m % B // GB
             e = small.tile([P, GB * SC, NC], F32)
-            nc.scalar.activation(out=e[:], in_=shifted[:], func=ACT.Exp)
+            nc.scalar.activation(out=e[:], in_=live[("shifted", g)][:], func=ACT.Exp)
             live[("e", g)] = e
 
-        def spread(g, bi):
-            c_n = live[("c", g)]
-            rep = reppool.tile([P, SC, NC, Q], F32)
-            nc.scalar.activation(
-                out=rep[:],
-                in_=c_n[:, bi * SC : (bi + 1) * SC, :].unsqueeze(3).to_broadcast([P, SC, NC, Q]),
-                func=ACT.Copy,
-            )
-            c_t = psum_b.tile([P, SC, P], F32, tag="b")
-            for c in range(SC):
-                nc.tensor.transpose(c_t[:, c, :], rep[:, c, :, :].rearrange("p n q -> p (n q)"), ident[:])
-            live[("c_t", g * GB + bi)] = c_t
-
-        def softmax_norm(g):
+        def normalise(m):
+            g = m % B // GB
             e = live[("e", g)]
             z = small.tile([P, GB * SC], F32)
             nc.vector.tensor_reduce(out=z[:], in_=e[:], axis=AX.X, op=ALU.add)
@@ -255,58 +329,47 @@ def tile_capsule_t_e_kernel(tc, inputs, W_words, W_scales, out):
                 out=c_n[:], in0=e[:], in1=rz[:].unsqueeze(2).to_broadcast([P, GB * SC, NC]), op=ALU.mult
             )
             live[("c", g)] = c_n
-            spread(g, 0)
 
-        def weighted_sums(g):
-            v = small.tile([P, NJ, GB], F32)
-            for bi in range(GB):
-                b = g * GB + bi
-                if bi + 1 < GB:
-                    spread(g, bi + 1)
-                for j in range(NJ):
-                    junk = junkpool.tile([P, S], F32)
-                    nc.vector.scalar_tensor_tensor(
-                        out=junk[:],
-                        in0=u[b][:, j, :],
-                        scalar=1.0,
-                        in1=live[("c_t", b)][:].rearrange("p c s -> p (c s)"),
-                        op0=ALU.mult,
-                        op1=ALU.mult,
-                        accum_out=v[:, j, bi : bi + 1],
-                    )
-            live[("v", g)] = v
-
-        steps = [(t - g, g) for t in range(PHASES + NG - 1) for g in range(NG)]
-
-        def valid(pos):
-            return 0 <= pos < len(steps) and 0 <= steps[pos][0] < PHASES
-
-        for pos in range(len(steps) + 2):
-            if valid(pos - 2):
-                phase, g = steps[pos - 2]
-                if phase % 2 == 1:
-                    softmax_norm(g)
-                else:
-                    squash(g, phase // 2)
-            if valid(pos - 1):
-                phase, g = steps[pos - 1]
-                if phase % 2 == 1:
-                    softmax_exp(g)
-                else:
-                    norm(g)
-            if valid(pos):
-                phase, g = steps[pos]
-                if phase == 0:
-                    project(g)
-                elif phase % 2 == 1:
-                    logit_products(g)
-                else:
-                    weighted_sums(g)
+        for n in range(-4, STEPS + 4):
+            if ends_group(n - 2):
+                inverse_root(n - 2)
+            if ends_group(n - 10) and feeds_a_round(n - 10):
+                exponent(n - 10)
+            if ends_group(n - 3):
+                squash(n - 3)
+            if ends_group(n - 11) and feeds_a_round(n - 11):
+                normalise(n - 11)
+            if in_later_round(n + 2):
+                replicate(n + 2)
+            if in_later_round(n + 1):
+                transpose_c(n + 1)
+            if in_round_0(n + 4):
+                load(n + 4)
+            if in_round_0(n + 1):
+                quantise(n + 1)
+            if in_round_0(n):
+                project(n)
+            if in_later_round(n):
+                sums(n)
+            if in_round_0(n + 2):
+                transpose_x(n + 2)
+            if feeds_a_round(n - 9):
+                logits(n - 9)
+                if ends_group(n - 9):
+                    shift(n - 9)
+            if ends_group(n):
+                square(n)
+            if feeds_a_round(n - 7):
+                products(n - 7)
+            if feeds_a_round(n - 8):
+                transpose_products(n - 8)
+            if ends_group(n - 1):
+                capsule_sums(n - 1)
 
         o_t = psum_s.tile([P, NJ, P], F32, tag="s")
         for j in range(NJ):
             nc.tensor.transpose(o_t[:, j, :], o_all[:, j * B : j * B + P], ident[:])
-        res = small.tile([B, NC * DC], F32)
+        res = const.tile([B, NC * DC], F32)
         nc.scalar.copy(
             out=res[:].rearrange("b (m j r) -> b m j r", j=NJ, r=R),
             in_=o_t[0:B].rearrange("b j (m r) -> b m j r", r=R),

@@ -255,35 +255,35 @@ def tile_capsule_t_e_kernel(tc, inputs, W_words, W_scales, out):
         def products(m):
             b = m % B
             prods = []
-            for j in range(NJ):
+            for j in (NJ - 2, 0, 1):
                 prod = prodpool.tile([P, S], F32)
-                if j % 2 == 0:
-                    nc.scalar.activation(
-                        out=prod[:], in_=u[b][:, j, :], func=ACT.Copy, scale=osum[b // GB][:, j, b % GB : b % GB + 1]
-                    )
-                else:
-                    nc.gpsimd.tensor_scalar(
-                        out=prod[:],
-                        in0=u[b][:, j, :],
-                        scalar1=osum[b // GB][:, j, b % GB : b % GB + 1],
-                        scalar2=0.0,
-                        op0=ALU.mult,
-                        op1=ALU.add,
-                    )
+                nc.scalar.activation(
+                    out=prod[:], in_=u[b][:, j, :], func=ACT.Copy, scale=osum[b // GB][:, j, b % GB : b % GB + 1]
+                )
                 prods.append(prod)
-            live[("prods", m)] = prods
+            last = prodpool.tile([P, S], F32, tag="prod")
+            nc.gpsimd.tensor_scalar(
+                out=last[:],
+                in0=u[b][:, NJ - 1, :],
+                scalar1=osum[b // GB][:, NJ - 1, b % GB : b % GB + 1],
+                scalar2=0.0,
+                op0=ALU.mult,
+                op1=ALU.add,
+            )
+            nc.gpsimd.tensor_tensor(out=last[:], in0=prods[0][:], in1=last[:], op=ALU.add)
+            live[("prods", m)] = [last, prods[1], prods[2]]
 
         def transpose_products(m):
             prods = live[("prods", m)]
             part = psum_a.tile([P, SC, P], F32, tag="a")
             for c in range(SC):
-                for j in range(NJ):
+                for k in range(len(prods)):
                     nc.tensor.matmul(
                         out=part[:, c, :],
-                        lhsT=prods[j][:, c * P : (c + 1) * P],
+                        lhsT=prods[k][:, c * P : (c + 1) * P],
                         rhs=ident[:],
-                        start=(j == 0),
-                        stop=(j == NJ - 1),
+                        start=(k == 0),
+                        stop=(k == len(prods) - 1),
                         is_transpose=True,
                     )
             live[("part", m)] = part

@@ -208,21 +208,24 @@ def tile_capsule_t_e_kernel(tc, inputs, W_words, W_scales, out):
                 )
                 live[("v", g)] = v_first
             v = live[("v", g)]
-            sq = small.tile([P, NJ, GB], F32)
-            nc.vector.tensor_tensor(out=sq[:], in0=v[:], in1=v[:], op=ALU.mult)
-            live[("sq", g)] = sq
+            sq = small.tile([P, GB, NJ], F32)
+            sq_sum = small.tile([P, GB], F32)
+            for bi in range(GB):
+                nc.scalar.activation(
+                    out=sq[:, bi, :], in_=v[:, :, bi], func=ACT.Square, accum_out=sq_sum[:, bi : bi + 1]
+                )
+            live[("sq", g)] = sq_sum
 
         def capsule_sums(m):
             g = m % B // GB
             ss = psum_s.tile([P, GB], F32, tag="s")
-            for j in range(NJ):
-                nc.tensor.matmul(
-                    out=ss[:],
-                    lhsT=same_capsule[:].rearrange("p n q -> p (n q)"),
-                    rhs=live[("sq", g)][:, j, :],
-                    start=(j == 0),
-                    stop=(j == NJ - 1),
-                )
+            nc.tensor.matmul(
+                out=ss[:],
+                lhsT=same_capsule[:].rearrange("p n q -> p (n q)"),
+                rhs=live[("sq", g)][:],
+                start=True,
+                stop=True,
+            )
             live[("ss", g)] = ss
 
         def inverse_root(m):
@@ -255,35 +258,35 @@ def tile_capsule_t_e_kernel(tc, inputs, W_words, W_scales, out):
         def products(m):
             b = m % B
             prods = []
-            for j in (NJ - 2, 0, 1):
+            for j in range(NJ):
                 prod = prodpool.tile([P, S], F32)
-                nc.scalar.activation(
-                    out=prod[:], in_=u[b][:, j, :], func=ACT.Copy, scale=osum[b // GB][:, j, b % GB : b % GB + 1]
-                )
+                if j % 2 == 0:
+                    nc.scalar.activation(
+                        out=prod[:], in_=u[b][:, j, :], func=ACT.Copy, scale=osum[b // GB][:, j, b % GB : b % GB + 1]
+                    )
+                else:
+                    nc.gpsimd.tensor_scalar(
+                        out=prod[:],
+                        in0=u[b][:, j, :],
+                        scalar1=osum[b // GB][:, j, b % GB : b % GB + 1],
+                        scalar2=0.0,
+                        op0=ALU.mult,
+                        op1=ALU.add,
+                    )
                 prods.append(prod)
-            last = prodpool.tile([P, S], F32, tag="prod")
-            nc.gpsimd.tensor_scalar(
-                out=last[:],
-                in0=u[b][:, NJ - 1, :],
-                scalar1=osum[b // GB][:, NJ - 1, b % GB : b % GB + 1],
-                scalar2=0.0,
-                op0=ALU.mult,
-                op1=ALU.add,
-            )
-            nc.gpsimd.tensor_tensor(out=last[:], in0=prods[0][:], in1=last[:], op=ALU.add)
-            live[("prods", m)] = [last, prods[1], prods[2]]
+            live[("prods", m)] = prods
 
         def transpose_products(m):
             prods = live[("prods", m)]
             part = psum_a.tile([P, SC, P], F32, tag="a")
             for c in range(SC):
-                for k in range(len(prods)):
+                for j in range(NJ):
                     nc.tensor.matmul(
                         out=part[:, c, :],
-                        lhsT=prods[k][:, c * P : (c + 1) * P],
+                        lhsT=prods[j][:, c * P : (c + 1) * P],
                         rhs=ident[:],
-                        start=(k == 0),
-                        stop=(k == len(prods) - 1),
+                        start=(j == 0),
+                        stop=(j == NJ - 1),
                         is_transpose=True,
                     )
             live[("part", m)] = part

@@ -260,7 +260,7 @@ def tile_capsule_t_e_kernel(tc, inputs, W_words, W_scales, out):
             prods = []
             for j in range(NJ):
                 prod = prodpool.tile([P, S], F32)
-                if j % 2 == 0:
+                if j % 2 == 0 or m >= B:
                     nc.scalar.activation(
                         out=prod[:], in_=u[b][:, j, :], func=ACT.Copy, scale=osum[b // GB][:, j, b % GB : b % GB + 1]
                     )

@@ -165,13 +165,16 @@ def tile_capsule_t_e_kernel(tc, inputs, W_words, W_scales, out):
 
         def replicate(m):
             bi = m % GB
-            c_n = live[("c", m % B // GB)]
+            e = live[("e", m % B // GB)]
+            rz = live[("rz", m % B // GB)]
             rep = reppool.tile([P, SC, NC, Q], F32)
-            nc.scalar.activation(
-                out=rep[:],
-                in_=c_n[:, bi * SC : (bi + 1) * SC, :].unsqueeze(3).to_broadcast([P, SC, NC, Q]),
-                func=ACT.Copy,
-            )
+            for c in range(SC):
+                nc.scalar.activation(
+                    out=rep[:, c, :, :],
+                    in_=e[:, bi * SC + c, :].unsqueeze(2).to_broadcast([P, NC, Q]),
+                    func=ACT.Copy,
+                    scale=rz[:, bi * SC + c : bi * SC + c + 1],
+                )
             live[("rep", m)] = rep
 
         def transpose_c(m):
@@ -242,13 +245,13 @@ def tile_capsule_t_e_kernel(tc, inputs, W_words, W_scales, out):
             v = live[("v", g)]
             rs_b = live[("rs", g)][:].unsqueeze(1).to_broadcast([P, NJ, GB])
             if rnd == 0:
-                nc.vector.tensor_tensor(out=osum[g][:], in0=v[:], in1=rs_b, op=ALU.mult)
+                nc.gpsimd.tensor_tensor(out=osum[g][:], in0=v[:], in1=rs_b, op=ALU.mult)
             elif rnd < ROUTINGS - 1:
                 o = small.tile([P, NJ, GB], F32)
-                nc.vector.tensor_tensor(out=o[:], in0=v[:], in1=rs_b, op=ALU.mult)
-                nc.vector.tensor_tensor(out=osum[g][:], in0=osum[g][:], in1=o[:], op=ALU.add)
+                nc.gpsimd.tensor_tensor(out=o[:], in0=v[:], in1=rs_b, op=ALU.mult)
+                nc.gpsimd.tensor_tensor(out=osum[g][:], in0=osum[g][:], in1=o[:], op=ALU.add)
             else:
-                nc.vector.tensor_tensor(
+                nc.gpsimd.tensor_tensor(
                     out=o_all[:, 0 : NJ * B].rearrange("p (j b) -> p j b", j=NJ)[:, :, g * GB : (g + 1) * GB],
                     in0=v[:],
                     in1=rs_b,
@@ -309,7 +312,7 @@ def tile_capsule_t_e_kernel(tc, inputs, W_words, W_scales, out):
             tmax = small.tile([P, GB * SC], F32)
             nc.vector.tensor_reduce(out=tmax[:], in_=t[:], axis=AX.X, op=ALU.max)
             shifted = small.tile([P, GB * SC, NC], F32)
-            nc.vector.tensor_tensor(
+            nc.gpsimd.tensor_tensor(
                 out=shifted[:], in0=t[:], in1=tmax[:].unsqueeze(2).to_broadcast([P, GB * SC, NC]), op=ALU.subtract
             )
             live[("shifted", g)] = shifted
@@ -327,11 +330,7 @@ def tile_capsule_t_e_kernel(tc, inputs, W_words, W_scales, out):
             nc.vector.tensor_reduce(out=z[:], in_=e[:], axis=AX.X, op=ALU.add)
             rz = small.tile([P, GB * SC], F32)
             nc.vector.reciprocal(out=rz[:], in_=z[:])
-            c_n = small.tile([P, GB * SC, NC], F32)
-            nc.vector.tensor_tensor(
-                out=c_n[:], in0=e[:], in1=rz[:].unsqueeze(2).to_broadcast([P, GB * SC, NC]), op=ALU.mult
-            )
-            live[("c", g)] = c_n
+            live[("rz", g)] = rz
 
         for n in range(-4, STEPS + 4):
             if ends_group(n - 2):

@@ -24,6 +24,7 @@ M = P // R
 GB = 4
 NG = B // GB
 STEPS = ROUTINGS * B
+EARLY = 2
 
 FLOPS = 2 * S * B * H * NC * DC + (2 * ROUTINGS - 1) * 2 * S * B * NC * DC
 
@@ -58,6 +59,16 @@ def tile_capsule_t_e_kernel(tc, inputs, W_words, W_scales, out):
         nc.vector.memset(o_all[:], 0.0)
         usum = const.tile([P, NJ, B], F32)
 
+        live = {}
+
+        def load(m):
+            x_b = xpool.tile([P, SC, H], BF16)
+            nc.sync.dma_start(out=x_b[:], in_=inputs[:, m, :].rearrange("(c p) h -> p c h", p=P))
+            live[("x", m)] = x_b
+
+        for m in range(EARLY):
+            load(m)
+
         w_raw = const.tile([P, NC * DC], U32)
         nc.sync.dma_start(out=w_raw[:].bitcast(I32), in_=W_words[0].rearrange("p n t -> p (n t)").bitcast(I32))
         plane_raw = const.tile([P, NC * DC], U8)
@@ -86,8 +97,6 @@ def tile_capsule_t_e_kernel(tc, inputs, W_words, W_scales, out):
         for g in range(NG):
             osum_g = const.tile([P, NJ, GB], F32, name="osum%d" % g)
             osum.append(osum_g)
-        live = {}
-
         def in_round_0(m):
             return 0 <= m < B
 
@@ -100,11 +109,6 @@ def tile_capsule_t_e_kernel(tc, inputs, W_words, W_scales, out):
         def feeds_a_round(m):
             return 0 <= m < STEPS - B
 
-        def load(m):
-            x_b = xpool.tile([P, SC, H], BF16)
-            nc.sync.dma_start(out=x_b[:], in_=inputs[:, m, :].rearrange("(c p) h -> p c h", p=P))
-            live[("x", m)] = x_b
-
         def transpose_x(m):
             x_b = live[("x", m)]
             grouped = qpool.tile([P, S, 4], BF16, align_bytes=64)
@@ -115,14 +119,9 @@ def tile_capsule_t_e_kernel(tc, inputs, W_words, W_scales, out):
                     for w in range(2):
                         nc.tensor.transpose(xt[:, c, w, :], words[:, w : H // 2 : 2], ident[:])
                 dst = grouped[:].bitcast(F32)[:, 2 * half * P : 2 * (half + 1) * P, :]
-                if half == 0:
-                    nc.scalar.copy(
-                        out=dst.rearrange("p (c s) w -> p c s w", c=2), in_=xt[:].rearrange("p c w s -> p c s w")
-                    )
-                else:
-                    nc.vector.tensor_copy(
-                        out=dst.rearrange("p (c s) w -> p c s w", c=2), in_=xt[:].rearrange("p c w s -> p c s w")
-                    )
+                nc.scalar.copy(
+                    out=dst.rearrange("p (c s) w -> p c s w", c=2), in_=xt[:].rearrange("p c w s -> p c s w")
+                )
             live[("grouped", m)] = grouped
 
         def quantise(m):
@@ -188,7 +187,7 @@ def tile_capsule_t_e_kernel(tc, inputs, W_words, W_scales, out):
             b = m % B
             if b % GB == 0:
                 v_new = small.tile([P, NJ, GB], F32, tag="v")
-                live[("v", b // GB)] = v_new
+                live[("v", b // GB)] = v_new[:]
             v = live[("v", b // GB)]
             for j in range(NJ):
                 junk = junkpool.tile([P, S], F32)
@@ -205,11 +204,7 @@ def tile_capsule_t_e_kernel(tc, inputs, W_words, W_scales, out):
         def square(m):
             g = m % B // GB
             if m < B:
-                v_first = small.tile([P, NJ, GB], F32, tag="v")
-                nc.vector.tensor_scalar(
-                    out=v_first[:], in0=usum[:, :, g * GB : (g + 1) * GB], scalar1=1.0 / NC, scalar2=None, op0=ALU.mult
-                )
-                live[("v", g)] = v_first
+                live[("v", g)] = usum[:, :, g * GB : (g + 1) * GB]
             v = live[("v", g)]
             sq = small.tile([P, GB, NJ], F32)
             sq_sum = small.tile([P, GB], F32)
@@ -234,7 +229,9 @@ def tile_capsule_t_e_kernel(tc, inputs, W_words, W_scales, out):
         def inverse_root(m):
             g = m % B // GB
             sse = small.tile([P, GB], F32)
-            nc.scalar.activation(out=sse[:], in_=live[("ss", g)][:], func=ACT.Copy, bias=1e-7)
+            nc.scalar.activation(
+                out=sse[:], in_=live[("ss", g)][:], func=ACT.Copy, bias=(NC * NC * 1e-7 if m < B else 1e-7)
+            )
             rs = small.tile([P, GB], F32)
             nc.gpsimd.tensor_tensor(out=rs[:], in0=sse[:], in1=neg_half[:], op=ALU.pow)
             live[("rs", g)] = rs
@@ -245,15 +242,15 @@ def tile_capsule_t_e_kernel(tc, inputs, W_words, W_scales, out):
             v = live[("v", g)]
             rs_b = live[("rs", g)][:].unsqueeze(1).to_broadcast([P, NJ, GB])
             if rnd == 0:
-                nc.gpsimd.tensor_tensor(out=osum[g][:], in0=v[:], in1=rs_b, op=ALU.mult)
+                nc.gpsimd.tensor_tensor(out=osum[g][:], in0=v, in1=rs_b, op=ALU.mult)
             elif rnd < ROUTINGS - 1:
                 o = small.tile([P, NJ, GB], F32)
-                nc.gpsimd.tensor_tensor(out=o[:], in0=v[:], in1=rs_b, op=ALU.mult)
+                nc.gpsimd.tensor_tensor(out=o[:], in0=v, in1=rs_b, op=ALU.mult)
                 nc.gpsimd.tensor_tensor(out=osum[g][:], in0=osum[g][:], in1=o[:], op=ALU.add)
             else:
                 nc.gpsimd.tensor_tensor(
                     out=o_all[:, 0 : NJ * B].rearrange("p (j b) -> p j b", j=NJ)[:, :, g * GB : (g + 1) * GB],
-                    in0=v[:],
+                    in0=v,
                     in1=rs_b,
                     op=ALU.mult,
                 )
@@ -263,7 +260,7 @@ def tile_capsule_t_e_kernel(tc, inputs, W_words, W_scales, out):
             prods = []
             for j in range(NJ):
                 prod = prodpool.tile([P, S], F32)
-                if j % 2 == 0 or m >= B:
+                if j == 0 or m >= B:
                     nc.scalar.activation(
                         out=prod[:], in_=u[b][:, j, :], func=ACT.Copy, scale=osum[b // GB][:, j, b % GB : b % GB + 1]
                     )
@@ -345,7 +342,7 @@ def tile_capsule_t_e_kernel(tc, inputs, W_words, W_scales, out):
                 replicate(n + 2)
             if in_later_round(n + 1):
                 transpose_c(n + 1)
-            if in_round_0(n + 4):
+            if in_round_0(n + 4) and n + 4 >= EARLY:
                 load(n + 4)
             if in_round_0(n + 1):
                 quantise(n + 1)

@@ -260,7 +260,7 @@ def tile_capsule_t_e_kernel(tc, inputs, W_words, W_scales, out):
             prods = []
             for j in range(NJ):
                 prod = prodpool.tile([P, S], F32)
-                if j == 0 or m >= B:
+                if j == 0 or (m >= B and j < NJ - 1):
                     nc.scalar.activation(
                         out=prod[:], in_=u[b][:, j, :], func=ACT.Copy, scale=osum[b // GB][:, j, b % GB : b % GB + 1]
                     )
@@ -306,27 +306,27 @@ def tile_capsule_t_e_kernel(tc, inputs, W_words, W_scales, out):
         def shift(m):
             g = m % B // GB
             t = live[("t", g)]
-            tmax = small.tile([P, GB * SC], F32)
-            nc.vector.tensor_reduce(out=tmax[:], in_=t[:], axis=AX.X, op=ALU.max)
-            shifted = small.tile([P, GB * SC, NC], F32)
-            nc.gpsimd.tensor_tensor(
-                out=shifted[:], in0=t[:], in1=tmax[:].unsqueeze(2).to_broadcast([P, GB * SC, NC]), op=ALU.subtract
-            )
-            live[("shifted", g)] = shifted
+            neg_max = small.tile([P, GB * SC], F32)
+            nc.vector.tensor_reduce(out=neg_max[:], in_=t[:], axis=AX.X, op=ALU.max, negate=True)
+            live[("neg_max", g)] = neg_max
 
         def exponent(m):
             g = m % B // GB
+            t = live[("t", g)]
+            neg_max = live[("neg_max", g)]
             e = small.tile([P, GB * SC, NC], F32)
-            nc.scalar.activation(out=e[:], in_=live[("shifted", g)][:], func=ACT.Exp)
+            z = small.tile([P, GB * SC], F32)
+            for i in range(GB * SC):
+                nc.scalar.activation(
+                    out=e[:, i, :], in_=t[:, i, :], func=ACT.Exp, bias=neg_max[:, i : i + 1], accum_out=z[:, i : i + 1]
+                )
             live[("e", g)] = e
+            live[("z", g)] = z
 
         def normalise(m):
             g = m % B // GB
-            e = live[("e", g)]
-            z = small.tile([P, GB * SC], F32)
-            nc.vector.tensor_reduce(out=z[:], in_=e[:], axis=AX.X, op=ALU.add)
             rz = small.tile([P, GB * SC], F32)
-            nc.vector.reciprocal(out=rz[:], in_=z[:])
+            nc.vector.reciprocal(out=rz[:], in_=live[("z", g)][:])
             live[("rz", g)] = rz
 
         for n in range(-4, STEPS + 4):

@@ -190,7 +190,7 @@ def tile_capsule_t_e_kernel(tc, inputs, W_words, W_scales, out):
                 live[("v", b // GB)] = v_new[:]
             v = live[("v", b // GB)]
             for j in range(NJ):
-                junk = junkpool.tile([P, S], F32)
+                junk = junkpool.tile([P, S], BF16)
                 nc.vector.scalar_tensor_tensor(
                     out=junk[:],
                     in0=u[b][:, j, :],
@@ -356,10 +356,10 @@ def tile_capsule_t_e_kernel(tc, inputs, W_words, W_scales, out):
                 logits(n - 9)
                 if ends_group(n - 9):
                     shift(n - 9)
-            if ends_group(n):
-                square(n)
             if feeds_a_round(n - 7):
                 products(n - 7)
+            if ends_group(n):
+                square(n)
             if feeds_a_round(n - 8):
                 transpose_products(n - 8)
             if ends_group(n - 1):

@@ -63,7 +63,14 @@ def tile_capsule_t_e_kernel(tc, inputs, W_words, W_scales, out):
 
         def load(m):
             x_b = xpool.tile([P, SC, H], BF16)
-            nc.sync.dma_start(out=x_b[:], in_=inputs[:, m, :].rearrange("(c p) h -> p c h", p=P))
+            x_view = inputs[:, m, :].rearrange("(c p) h -> p c h", p=P)
+            if m == 0:
+                for half in range(SC // 2):
+                    nc.sync.dma_start(
+                        out=x_b[:, 2 * half : 2 * half + 2, :], in_=x_view[:, 2 * half : 2 * half + 2, :]
+                    )
+            else:
+                nc.sync.dma_start(out=x_b[:], in_=x_view)
             live[("x", m)] = x_b
 
         for m in range(EARLY):

@@ -190,13 +190,13 @@ def tile_capsule_t_e_kernel(tc, inputs, W_words, W_scales, out):
                 nc.tensor.transpose(c_t[:, c, :], rep[:, c, :, :].rearrange("p n q -> p (n q)"), ident[:])
             live[("c_t", m)] = c_t
 
-        def sums(m):
+        def sums(m, blocks):
             b = m % B
-            if b % GB == 0:
+            if b % GB == 0 and 0 in blocks:
                 v_new = small.tile([P, NJ, GB], F32, tag="v")
                 live[("v", b // GB)] = v_new[:]
             v = live[("v", b // GB)]
-            for j in range(NJ):
+            for j in blocks:
                 junk = junkpool.tile([P, S], BF16)
                 nc.vector.scalar_tensor_tensor(
                     out=junk[:],
@@ -356,13 +356,17 @@ def tile_capsule_t_e_kernel(tc, inputs, W_words, W_scales, out):
             if in_round_0(n):
                 project(n)
             if in_later_round(n):
-                sums(n)
+                sums(n, range(NJ - 2))
             if in_round_0(n + 2):
                 transpose_x(n + 2)
             if feeds_a_round(n - 9):
                 logits(n - 9)
-                if ends_group(n - 9):
-                    shift(n - 9)
+            if in_later_round(n):
+                sums(n, range(NJ - 2, NJ - 1))
+            if ends_group(n - 9) and feeds_a_round(n - 9):
+                shift(n - 9)
+            if in_later_round(n):
+                sums(n, range(NJ - 1, NJ))
             if feeds_a_round(n - 7):
                 products(n - 7)
             if ends_group(n):

@@ -24,6 +24,7 @@ M = P // R
 GB = 4
 NG = B // GB
 STEPS = ROUTINGS * B
+APART = (0, 2)
 EARLY = 2
 
 FLOPS = 2 * S * B * H * NC * DC + (2 * ROUTINGS - 1) * 2 * S * B * NC * DC
@@ -37,6 +38,7 @@ def tile_capsule_t_e_kernel(tc, inputs, W_words, W_scales, out):
         xpool = ctx.enter_context(tc.tile_pool(name="xpool", bufs=4))
         qpool = ctx.enter_context(tc.tile_pool(name="qpool", bufs=2))
         prodpool = ctx.enter_context(tc.tile_pool(name="prodpool", bufs=2 * NJ))
+        weighpool = ctx.enter_context(tc.tile_pool(name="weighpool", bufs=3))
         reppool = ctx.enter_context(tc.tile_pool(name="reppool", bufs=2))
         junkpool = ctx.enter_context(tc.tile_pool(name="junkpool", bufs=4))
         small = ctx.enter_context(tc.tile_pool(name="small", bufs=3))
@@ -110,6 +112,9 @@ def tile_capsule_t_e_kernel(tc, inputs, W_words, W_scales, out):
         def in_later_round(m):
             return B <= m < STEPS
 
+        def apart(m):
+            return m % GB in APART
+
         def ends_group(m):
             return 0 <= m < STEPS and m % GB == GB - 1
 
@@ -169,6 +174,69 @@ def tile_capsule_t_e_kernel(tc, inputs, W_words, W_scales, out):
                         accum_out=usum[:, j, m : m + 1],
                     )
 
+        def project_turned(m):
+            codes, plane = live[("codes", m)]
+            acc = psum_s.tile([P, SC, P], F32, tag="s")
+            for c in range(SC):
+                nc.tensor.matmul_mx(
+                    out=acc[:, c, :],
+                    lhsT=codes[:, c * P : (c + 1) * P].bitcast(FP8X4),
+                    lhsT_scale=plane[:, c * P : (c + 1) * P],
+                    rhs=w_words[:, (NJ - 1) * P : NJ * P].bitcast(FP8X4),
+                    rhs_scale=w_plane[:, (NJ - 1) * P : NJ * P],
+                    start=True,
+                    stop=True,
+                )
+            u_turned = upool.tile([P, SC, P], F32, name="u_turned%d" % m)
+            nc.vector.tensor_copy(out=u_turned[:], in_=acc[:])
+            live[("u_turned", m)] = u_turned
+
+        def couple(m):
+            g = m % B // GB
+            c = small.tile([P, GB * SC, NC], F32)
+            nc.gpsimd.tensor_tensor(
+                out=c[:],
+                in0=live[("e", g)][:],
+                in1=live[("rz", g)][:].unsqueeze(2).to_broadcast([P, GB * SC, NC]),
+                op=ALU.mult,
+            )
+            live[("c", g)] = c
+
+        def weigh(m):
+            bi = m % GB
+            weighed = weighpool.tile([P, SC, NC, Q], F32)
+            nc.gpsimd.tensor_tensor(
+                out=weighed[:],
+                in0=live[("u_turned", m % B)][:].rearrange("p c (n q) -> p c n q", q=Q),
+                in1=live[("c", m % B // GB)][:, bi * SC : (bi + 1) * SC, :].unsqueeze(3).to_broadcast([P, SC, NC, Q]),
+                op=ALU.mult,
+            )
+            live[("weighed", m)] = weighed
+
+        def turn_back(m):
+            i = APART.index(m % GB)
+            if i == 0:
+                turned = psum_s.tile([P, len(APART), P], F32, tag="s")
+                live["turned"] = turned
+            for c in range(SC):
+                nc.tensor.matmul(
+                    out=live["turned"][:, i, :],
+                    lhsT=live[("weighed", m)][:, c, :, :].rearrange("p n q -> p (n q)"),
+                    rhs=ident[:],
+                    start=(c == 0),
+                    stop=(c == SC - 1),
+                    is_transpose=True,
+                )
+
+        def add_up(m):
+            g = m % B // GB
+            nc.vector.tensor_reduce(
+                out=live[("v", g)][:, NJ - 1, APART[0] : APART[-1] + 1 : APART[1] - APART[0]],
+                in_=live["turned"][:],
+                axis=AX.X,
+                op=ALU.add,
+            )
+
         def replicate(m):
             bi = m % GB
             e = live[("e", m % B // GB)]
@@ -197,6 +265,8 @@ def tile_capsule_t_e_kernel(tc, inputs, W_words, W_scales, out):
                 live[("v", b // GB)] = v_new[:]
             v = live[("v", b // GB)]
             for j in blocks:
+                if apart(m) and j == NJ - 1:
+                    continue
                 junk = junkpool.tile([P, S], BF16)
                 nc.vector.scalar_tensor_tensor(
                     out=junk[:],
@@ -223,7 +293,7 @@ def tile_capsule_t_e_kernel(tc, inputs, W_words, W_scales, out):
 
         def capsule_sums(m):
             g = m % B // GB
-            ss = psum_s.tile([P, GB], F32, tag="s")
+            ss = psum_a.tile([P, GB], F32, tag="a")
             nc.tensor.matmul(
                 out=ss[:],
                 lhsT=same_capsule[:].rearrange("p n q -> p (n q)"),
@@ -267,7 +337,7 @@ def tile_capsule_t_e_kernel(tc, inputs, W_words, W_scales, out):
             prods = []
             for j in range(NJ):
                 prod = prodpool.tile([P, S], F32)
-                if j == 0 or (m >= B and j < NJ - 1):
+                if j == 0 or (m >= 9 and j < NJ - 1):
                     nc.scalar.activation(
                         out=prod[:], in_=u[b][:, j, :], func=ACT.Copy, scale=osum[b // GB][:, j, b % GB : b % GB + 1]
                     )
@@ -322,12 +392,14 @@ def tile_capsule_t_e_kernel(tc, inputs, W_words, W_scales, out):
             t = live[("t", g)]
             neg_max = live[("neg_max", g)]
             e = small.tile([P, GB * SC, NC], F32)
-            z = small.tile([P, GB * SC], F32)
             for i in range(GB * SC):
-                nc.scalar.activation(
-                    out=e[:, i, :], in_=t[:, i, :], func=ACT.Exp, bias=neg_max[:, i : i + 1], accum_out=z[:, i : i + 1]
-                )
+                nc.scalar.activation(out=e[:, i, :], in_=t[:, i, :], func=ACT.Exp, bias=neg_max[:, i : i + 1])
             live[("e", g)] = e
+
+        def exponent_sum(m):
+            g = m % B // GB
+            z = small.tile([P, GB * SC], F32)
+            nc.vector.tensor_reduce(out=z[:], in_=live[("e", g)][:], axis=AX.X, op=ALU.add)
             live[("z", g)] = z
 
         def normalise(m):
@@ -355,22 +427,34 @@ def tile_capsule_t_e_kernel(tc, inputs, W_words, W_scales, out):
                 quantise(n + 1)
             if in_round_0(n):
                 project(n)
+                if apart(n):
+                    project_turned(n)
             if in_later_round(n):
                 sums(n, range(NJ - 2))
             if in_round_0(n + 2):
                 transpose_x(n + 2)
             if feeds_a_round(n - 9):
                 logits(n - 9)
+            if ends_group(n - 10) and feeds_a_round(n - 10):
+                exponent_sum(n - 10)
             if in_later_round(n):
                 sums(n, range(NJ - 2, NJ - 1))
             if ends_group(n - 9) and feeds_a_round(n - 9):
                 shift(n - 9)
+            if in_later_round(n) and n % GB == APART[-1] + 1:
+                add_up(n)
             if in_later_round(n):
                 sums(n, range(NJ - 1, NJ))
+            if ends_group(n - 11) and feeds_a_round(n - 11):
+                couple(n - 11)
             if feeds_a_round(n - 7):
                 products(n - 7)
+            if in_later_round(n + 1) and apart(n + 1):
+                weigh(n + 1)
             if ends_group(n):
                 square(n)
+            if in_later_round(n) and apart(n):
+                turn_back(n)
             if feeds_a_round(n - 8):
                 transpose_products(n - 8)
             if ends_group(n - 1):

@@ -24,7 +24,7 @@ M = P // R
 GB = 4
 NG = B // GB
 STEPS = ROUTINGS * B
-APART = (0, 2)
+APART = (0, 1, 2)
 EARLY = 2
 
 FLOPS = 2 * S * B * H * NC * DC + (2 * ROUTINGS - 1) * 2 * S * B * NC * DC
@@ -242,6 +242,16 @@ def tile_capsule_t_e_kernel(tc, inputs, W_words, W_scales, out):
             e = live[("e", m % B // GB)]
             rz = live[("rz", m % B // GB)]
             rep = reppool.tile([P, SC, NC, Q], F32)
+            if bi > 0:
+                nc.scalar.copy(
+                    out=rep[:].rearrange("p c n q -> p (c n) q"),
+                    in_=live[("c", m % B // GB)][:, bi * SC : (bi + 1) * SC, :]
+                    .rearrange("p c n -> p (c n)")
+                    .unsqueeze(2)
+                    .to_broadcast([P, SC * NC, Q]),
+                )
+                live[("rep", m)] = rep
+                return
             for c in range(SC):
                 nc.scalar.activation(
                     out=rep[:, c, :, :],

from contextlib import ExitStack

import concourse.mybir as mybir
from concourse.masks import make_identity

F32 = mybir.dt.float32
BF16 = mybir.dt.bfloat16
I32 = mybir.dt.int32
U32 = mybir.dt.uint32
U8 = mybir.dt.uint8
FP8X4 = mybir.dt.float8_e4m3fn_x4
ALU = mybir.AluOpType
ACT = mybir.ActivationFunctionType
AX = mybir.AxisListType

S, B, H, NC, DC = 512, 16, 512, 8, 64
ROUTINGS = 4
P = 128
SC = S // P
NJ = NC * DC // P
Q = P // NC
R = 4
M = P // R
GB = 4
NG = B // GB
STEPS = ROUTINGS * B
APART = (0, 1, 2)
EARLY = 2

FLOPS = 2 * S * B * H * NC * DC + (2 * ROUTINGS - 1) * 2 * S * B * NC * DC


def tile_capsule_t_e_kernel(tc, inputs, W_words, W_scales, out):
    nc = tc.nc
    with ExitStack() as ctx:
        const = ctx.enter_context(tc.tile_pool(name="const", bufs=1))
        upool = ctx.enter_context(tc.tile_pool(name="upool", bufs=1))
        xpool = ctx.enter_context(tc.tile_pool(name="xpool", bufs=4))
        qpool = ctx.enter_context(tc.tile_pool(name="qpool", bufs=2))
        prodpool = ctx.enter_context(tc.tile_pool(name="prodpool", bufs=2 * NJ))
        weighpool = ctx.enter_context(tc.tile_pool(name="weighpool", bufs=3))
        reppool = ctx.enter_context(tc.tile_pool(name="reppool", bufs=2))
        junkpool = ctx.enter_context(tc.tile_pool(name="junkpool", bufs=4))
        small = ctx.enter_context(tc.tile_pool(name="small", bufs=3))
        psum_a = ctx.enter_context(tc.psum_pool(name="psum_a", bufs=4))
        psum_b = ctx.enter_context(tc.psum_pool(name="psum_b", bufs=3))
        psum_s = ctx.enter_context(tc.psum_pool(name="psum_s", bufs=1))
        ctx.enter_context(tc.manual_schedule())

        ident = const.tile([P, P], F32)
        make_identity(nc, ident[:])
        capsule_of = const.tile([P, NC], F32)
        nc.vector.tensor_reduce(
            out=capsule_of[:], in_=ident[:].rearrange("p (n q) -> p n q", q=Q), axis=AX.X, op=ALU.add
        )
        same_capsule = const.tile([P, NC, Q], F32)
        nc.vector.tensor_copy(out=same_capsule[:], in_=capsule_of[:].unsqueeze(2).to_broadcast([P, NC, Q]))
        neg_half = const.tile([P, GB], F32)
        nc.vector.memset(neg_half[:], -0.5)
        o_all = const.tile([P, (NJ - 1) * B + P], F32)
        nc.vector.memset(o_all[:], 0.0)
        usum = const.tile([P, NJ, B], F32)

        live = {}

        def load(m):
            x_b = xpool.tile([P, SC, H], BF16)
            x_view = inputs[:, m, :].rearrange("(c p) h -> p c h", p=P)
            if m == 0:
                for half in range(SC // 2):
                    nc.sync.dma_start(
                        out=x_b[:, 2 * half : 2 * half + 2, :], in_=x_view[:, 2 * half : 2 * half + 2, :]
                    )
            else:
                nc.sync.dma_start(out=x_b[:], in_=x_view)
            live[("x", m)] = x_b

        for m in range(EARLY):
            load(m)

        w_raw = const.tile([P, NC * DC], U32)
        nc.sync.dma_start(out=w_raw[:].bitcast(I32), in_=W_words[0].rearrange("p n t -> p (n t)").bitcast(I32))
        plane_raw = const.tile([P, NC * DC], U8)
        nc.vector.memset(plane_raw[:].bitcast(I32), 0)
        for quad in range(4):
            nc.sync.dma_start(
                out=plane_raw[32 * quad : 32 * quad + 4, :].bitcast(I32),
                in_=W_scales[0, 4 * quad : 4 * quad + 4, :].bitcast(I32),
            )
        w_words = const.tile([P, NC * DC], U32, align_bytes=64)
        nc.vector.tensor_copy(
            out=w_words[:].bitcast(I32).rearrange("p (j m r) -> p j m r", j=NJ, r=R),
            in_=w_raw[:].bitcast(I32).rearrange("p (m j r) -> p j m r", j=NJ, r=R),
        )
        w_plane = const.tile([P, NC * DC], U8, align_bytes=64)
        nc.vector.tensor_copy(
            out=w_plane[:].bitcast(I32).rearrange("p (j m) -> p j m", j=NJ),
            in_=plane_raw[:].bitcast(I32).rearrange("p (m j) -> p j m", j=NJ),
        )

        u = []
        for b in range(B):
            u_b = upool.tile([P, NJ, S], F32, name="u%d" % b)
            u.append(u_b)
        osum = []
        for g in range(NG):
            osum_g = const.tile([P, NJ, GB], F32, name="osum%d" % g)
            osum.append(osum_g)
        def in_round_0(m):
            return 0 <= m < B

        def in_later_round(m):
            return B <= m < STEPS

        def apart(m):
            return m % GB in APART

        def ends_group(m):
            return 0 <= m < STEPS and m % GB == GB - 1

        def feeds_a_round(m):
            return 0 <= m < STEPS - B

        def transpose_x(m):
            x_b = live[("x", m)]
            grouped = qpool.tile([P, S, 4], BF16, align_bytes=64)
            for half in range(SC // 2):
                xt = psum_b.tile([P, 2, 2, P], F32, tag="b")
                for c in range(2):
                    words = x_b[:, 2 * half + c, :].bitcast(F32)
                    for w in range(2):
                        nc.tensor.transpose(xt[:, c, w, :], words[:, w : H // 2 : 2], ident[:])
                dst = grouped[:].bitcast(F32)[:, 2 * half * P : 2 * (half + 1) * P, :]
                nc.scalar.copy(
                    out=dst.rearrange("p (c s) w -> p c s w", c=2), in_=xt[:].rearrange("p c w s -> p c s w")
                )
            live[("grouped", m)] = grouped

        def quantise(m):
            codes = qpool.tile([P, S], U32, align_bytes=64)
            plane = qpool.tile([P, S], U8, align_bytes=64)
            nc.vector.quantize_mx(
                out=codes[:].bitcast(FP8X4),
                scales=plane[:],
                in_=live[("grouped", m)][:].rearrange("p s t -> p (s t)"),
            )
            live[("codes", m)] = (codes, plane)

        def project(m):
            codes, plane = live[("codes", m)]
            for j in range(NJ):
                acc = psum_a.tile([P, S], F32, tag="a")
                nc.tensor.matmul_mx(
                    out=acc[:],
                    lhsT=w_words[:, j * P : (j + 1) * P].bitcast(FP8X4),
                    lhsT_scale=w_plane[:, j * P : (j + 1) * P],
                    rhs=codes[:].bitcast(FP8X4),
                    rhs_scale=plane[:],
                    start=True,
                    stop=True,
                )
                if j % 2 == 0:
                    nc.scalar.activation(
                        out=u[m][:, j, :], in_=acc[:], func=ACT.Copy, accum_out=usum[:, j, m : m + 1]
                    )
                else:
                    nc.vector.tensor_scalar(
                        out=u[m][:, j, :],
                        in0=acc[:],
                        scalar1=1.0,
                        scalar2=None,
                        op0=ALU.mult,
                        op1=ALU.add,
                        accum_out=usum[:, j, m : m + 1],
                    )

        def project_turned(m):
            codes, plane = live[("codes", m)]
            acc = psum_s.tile([P, SC, P], F32, tag="s")
            for c in range(SC):
                nc.tensor.matmul_mx(
                    out=acc[:, c, :],
                    lhsT=codes[:, c * P : (c + 1) * P].bitcast(FP8X4),
                    lhsT_scale=plane[:, c * P : (c + 1) * P],
                    rhs=w_words[:, (NJ - 1) * P : NJ * P].bitcast(FP8X4),
                    rhs_scale=w_plane[:, (NJ - 1) * P : NJ * P],
                    start=True,
                    stop=True,
                )
            u_turned = upool.tile([P, SC, P], F32, name="u_turned%d" % m)
            nc.vector.tensor_copy(out=u_turned[:], in_=acc[:])
            live[("u_turned", m)] = u_turned

        def couple(m):
            g = m % B // GB
            c = small.tile([P, GB * SC, NC], F32)
            nc.gpsimd.tensor_tensor(
                out=c[:],
                in0=live[("e", g)][:],
                in1=live[("rz", g)][:].unsqueeze(2).to_broadcast([P, GB * SC, NC]),
                op=ALU.mult,
            )
            live[("c", g)] = c

        def weigh(m):
            bi = m % GB
            weighed = weighpool.tile([P, SC, NC, Q], F32)
            nc.gpsimd.tensor_tensor(
                out=weighed[:],
                in0=live[("u_turned", m % B)][:].rearrange("p c (n q) -> p c n q", q=Q),
                in1=live[("c", m % B // GB)][:, bi * SC : (bi + 1) * SC, :].unsqueeze(3).to_broadcast([P, SC, NC, Q]),
                op=ALU.mult,
            )
            live[("weighed", m)] = weighed

        def turn_back(m):
            i = APART.index(m % GB)
            if i == 0:
                turned = psum_s.tile([P, len(APART), P], F32, tag="s")
                live["turned"] = turned
            for c in range(SC):
                nc.tensor.matmul(
                    out=live["turned"][:, i, :],
                    lhsT=live[("weighed", m)][:, c, :, :].rearrange("p n q -> p (n q)"),
                    rhs=ident[:],
                    start=(c == 0),
                    stop=(c == SC - 1),
                    is_transpose=True,
                )

        def add_up(m):
            g = m % B // GB
            nc.vector.tensor_reduce(
                out=live[("v", g)][:, NJ - 1, APART[0] : APART[-1] + 1 : APART[1] - APART[0]],
                in_=live["turned"][:],
                axis=AX.X,
                op=ALU.add,
            )

        def replicate(m):
            bi = m % GB
            e = live[("e", m % B // GB)]
            rz = live[("rz", m % B // GB)]
            rep = reppool.tile([P, SC, NC, Q], F32)
            if bi > 0:
                nc.scalar.copy(
                    out=rep[:].rearrange("p c n q -> p (c n) q"),
                    in_=live[("c", m % B // GB)][:, bi * SC : (bi + 1) * SC, :]
                    .rearrange("p c n -> p (c n)")
                    .unsqueeze(2)
                    .to_broadcast([P, SC * NC, Q]),
                )
                live[("rep", m)] = rep
                return
            for c in range(SC):
                nc.scalar.activation(
                    out=rep[:, c, :, :],
                    in_=e[:, bi * SC + c, :].unsqueeze(2).to_broadcast([P, NC, Q]),
                    func=ACT.Copy,
                    scale=rz[:, bi * SC + c : bi * SC + c + 1],
                )
            live[("rep", m)] = rep

        def transpose_c(m):
            rep = live[("rep", m)]
            c_t = psum_b.tile([P, SC, P], F32, tag="b")
            for c in range(SC):
                nc.tensor.transpose(c_t[:, c, :], rep[:, c, :, :].rearrange("p n q -> p (n q)"), ident[:])
            live[("c_t", m)] = c_t

        def sums(m, blocks):
            b = m % B
            if b % GB == 0 and 0 in blocks:
                v_new = small.tile([P, NJ, GB], F32, tag="v")
                live[("v", b // GB)] = v_new[:]
            v = live[("v", b // GB)]
            for j in blocks:
                if apart(m) and j == NJ - 1:
                    continue
                junk = junkpool.tile([P, S], BF16)
                nc.vector.scalar_tensor_tensor(
                    out=junk[:],
                    in0=u[b][:, j, :],
                    scalar=1.0,
                    in1=live[("c_t", m)][:].rearrange("p c s -> p (c s)"),
                    op0=ALU.mult,
                    op1=ALU.mult,
                    accum_out=v[:, j, b % GB : b % GB + 1],
                )

        def square(m):
            g = m % B // GB
            if m < B:
                live[("v", g)] = usum[:, :, g * GB : (g + 1) * GB]
            v = live[("v", g)]
            sq = small.tile([P, GB, NJ], F32)
            sq_sum = small.tile([P, GB], F32)
            for bi in range(GB):
                nc.scalar.activation(
                    out=sq[:, bi, :], in_=v[:, :, bi], func=ACT.Square, accum_out=sq_sum[:, bi : bi + 1]
                )
            live[("sq", g)] = sq_sum

        def capsule_sums(m):
            g = m % B // GB
            ss = psum_a.tile([P, GB], F32, tag="a")
            nc.tensor.matmul(
                out=ss[:],
                lhsT=same_capsule[:].rearrange("p n q -> p (n q)"),
                rhs=live[("sq", g)][:],
                start=True,
                stop=True,
            )
            live[("ss", g)] = ss

        def inverse_root(m):
            g = m % B // GB
            sse = small.tile([P, GB], F32)
            nc.scalar.activation(
                out=sse[:], in_=live[("ss", g)][:], func=ACT.Copy, bias=(NC * NC * 1e-7 if m < B else 1e-7)
            )
            rs = small.tile([P, GB], F32)
            nc.gpsimd.tensor_tensor(out=rs[:], in0=sse[:], in1=neg_half[:], op=ALU.pow)
            live[("rs", g)] = rs

        def squash(m):
            g = m % B // GB
            rnd = m // B
            v = live[("v", g)]
            rs_b = live[("rs", g)][:].unsqueeze(1).to_broadcast([P, NJ, GB])
            if rnd == 0:
                nc.gpsimd.tensor_tensor(out=osum[g][:], in0=v, in1=rs_b, op=ALU.mult)
            elif rnd < ROUTINGS - 1:
                o = small.tile([P, NJ, GB], F32)
                nc.gpsimd.tensor_tensor(out=o[:], in0=v, in1=rs_b, op=ALU.mult)
                nc.gpsimd.tensor_tensor(out=osum[g][:], in0=osum[g][:], in1=o[:], op=ALU.add)
            else:
                nc.gpsimd.tensor_tensor(
                    out=o_all[:, 0 : NJ * B].rearrange("p (j b) -> p j b", j=NJ)[:, :, g * GB : (g + 1) * GB],
                    in0=v,
                    in1=rs_b,
                    op=ALU.mult,
                )

        def products(m):
            b = m % B
            prods = []
            for j in range(NJ):
                prod = prodpool.tile([P, S], F32)
                if j == 0 or (m >= 9 and j < NJ - 1):
                    nc.scalar.activation(
                        out=prod[:], in_=u[b][:, j, :], func=ACT.Copy, scale=osum[b // GB][:, j, b % GB : b % GB + 1]
                    )
                else:
                    nc.gpsimd.tensor_scalar(
                        out=prod[:],
                        in0=u[b][:, j, :],
                        scalar1=osum[b // GB][:, j, b % GB : b % GB + 1],
                        scalar2=0.0,
                        op0=ALU.mult,
                        op1=ALU.add,
                    )
                prods.append(prod)
            live[("prods", m)] = prods

        def transpose_products(m):
            prods = live[("prods", m)]
            part = psum_a.tile([P, SC, P], F32, tag="a")
            for c in range(SC):
                for j in range(NJ):
                    nc.tensor.matmul(
                        out=part[:, c, :],
                        lhsT=prods[j][:, c * P : (c + 1) * P],
                        rhs=ident[:],
                        start=(j == 0),
                        stop=(j == NJ - 1),
                        is_transpose=True,
                    )
            live[("part", m)] = part

        def logits(m):
            b = m % B
            if b % GB == 0:
                t_new = small.tile([P, GB * SC, NC], F32, tag="t")
                live[("t", b // GB)] = t_new
            nc.vector.tensor_reduce(
                out=live[("t", b // GB)][:, b % GB * SC : (b % GB + 1) * SC, :],
                in_=live[("part", m)][:].rearrange("p c (n q) -> p c n q", q=Q),
                axis=AX.X,
                op=ALU.add,
            )

        def shift(m):
            g = m % B // GB
            t = live[("t", g)]
            neg_max = small.tile([P, GB * SC], F32)
            nc.vector.tensor_reduce(out=neg_max[:], in_=t[:], axis=AX.X, op=ALU.max, negate=True)
            live[("neg_max", g)] = neg_max

        def exponent(m):
            g = m % B // GB
            t = live[("t", g)]
            neg_max = live[("neg_max", g)]
            e = small.tile([P, GB * SC, NC], F32)
            for i in range(GB * SC):
                nc.scalar.activation(out=e[:, i, :], in_=t[:, i, :], func=ACT.Exp, bias=neg_max[:, i : i + 1])
            live[("e", g)] = e

        def exponent_sum(m):
            g = m % B // GB
            z = small.tile([P, GB * SC], F32)
            nc.vector.tensor_reduce(out=z[:], in_=live[("e", g)][:], axis=AX.X, op=ALU.add)
            live[("z", g)] = z

        def normalise(m):
            g = m % B // GB
            rz = small.tile([P, GB * SC], F32)
            nc.vector.reciprocal(out=rz[:], in_=live[("z", g)][:])
            live[("rz", g)] = rz

        for n in range(-4, STEPS + 4):
            if ends_group(n - 2):
                inverse_root(n - 2)
            if ends_group(n - 10) and feeds_a_round(n - 10):
                exponent(n - 10)
            if ends_group(n - 3):
                squash(n - 3)
            if ends_group(n - 11) and feeds_a_round(n - 11):
                normalise(n - 11)
            if in_later_round(n + 2):
                replicate(n + 2)
            if in_later_round(n + 1):
                transpose_c(n + 1)
            if in_round_0(n + 4) and n + 4 >= EARLY:
                load(n + 4)
            if in_round_0(n + 1):
                quantise(n + 1)
            if in_round_0(n):
                project(n)
                if apart(n):
                    project_turned(n)
            if in_later_round(n):
                sums(n, range(NJ - 2))
            if in_round_0(n + 2):
                transpose_x(n + 2)
            if feeds_a_round(n - 9):
                logits(n - 9)
            if ends_group(n - 10) and feeds_a_round(n - 10):
                exponent_sum(n - 10)
            if in_later_round(n):
                sums(n, range(NJ - 2, NJ - 1))
            if ends_group(n - 9) and feeds_a_round(n - 9):
                shift(n - 9)
            if in_later_round(n) and n % GB == APART[-1] + 1:
                add_up(n)
            if in_later_round(n):
                sums(n, range(NJ - 1, NJ))
            if ends_group(n - 11) and feeds_a_round(n - 11):
                couple(n - 11)
            if feeds_a_round(n - 7):
                products(n - 7)
            if in_later_round(n + 1) and apart(n + 1):
                weigh(n + 1)
            if ends_group(n):
                square(n)
            if in_later_round(n) and apart(n):
                turn_back(n)
            if feeds_a_round(n - 8):
                transpose_products(n - 8)
            if ends_group(n - 1):
                capsule_sums(n - 1)

        o_t = psum_s.tile([P, NJ, P], F32, tag="s")
        for j in range(NJ):
            nc.tensor.transpose(o_t[:, j, :], o_all[:, j * B : j * B + P], ident[:])
        res = const.tile([B, NC * DC], F32)
        nc.scalar.copy(
            out=res[:].rearrange("b (m j r) -> b m j r", j=NJ, r=R),
            in_=o_t[0:B].rearrange("b j (m r) -> b m j r", r=R),
        )
        nc.sync.dma_start(out=out.rearrange("b n d -> b (n d)"), in_=res[:])
